import numpy as np
import ml_dtypes

BF16 = ml_dtypes.bfloat16


def bf(x):
    return np.asarray(x, np.float32).astype(BF16)


def f32(x):
    return np.asarray(x, np.float32)


def f64(x):
    return np.asarray(x).astype(np.float64)


def striped(idx):
    return np.tile(idx.reshape(-1, 16).T, (8, 1))


K, C, S, N = 128, 256, 2048, 3072


def setup_inputs():
    return {
        "self_h": f32(np.random.standard_normal((C, S))),
        "src_e": bf(np.random.standard_normal((K, N))),
        "w": bf(np.random.standard_normal((K, C)) / np.sqrt(K)),
        "b": f32(0.1 * np.random.standard_normal((C, 1))),
        "wa_z": f32(0.5 * np.random.standard_normal((C, 1))),
        "wa_s": f32(0.5 * np.random.standard_normal((C, 1))),
        "offs": striped(np.random.permutation(np.tile(np.arange(S), 2))[:N]),
    }


def reference(self_h, src_e, w, b, wa_z, wa_s, offs):
    idx = offs[:16].T.reshape(-1)
    hs = f64(self_h) * f64(wa_s)
    zt = (f64(w).T @ f64(src_e) + f64(b)) * f64(wa_z)
    return hs[:, idx] + zt

@@ -1,0 +1,83 @@
+import concourse.mybir as mybir
+from concourse.masks import make_identity
+
+P = 128
+K, C, S, N = 128, 256, 2048, 3072
+BLOCKS = C // P
+PIECE = 1024
+BANK = 512
+PER_COLUMN = 16
+
+FLOPS = 2 * K * C * N
+
+F32, BF16, U16 = mybir.dt.float32, mybir.dt.bfloat16, mybir.dt.uint16
+ADD = mybir.AluOpType.add
+IDENTITY = mybir.ActivationFunctionType.Identity
+
+
+def tile_reledgeupdate_kernel(tc, self_h, src_e, w, b, wa_z, wa_s, offs, out):
+    nc = tc.nc
+    with (
+        tc.tile_pool(name="held", bufs=1) as held,
+        tc.tile_pool(name="ring", bufs=3) as ring,
+        tc.psum_pool(name="flip", bufs=1) as flip,
+        tc.psum_pool(name="banks", bufs=4) as banks,
+    ):
+        offsets = held.tile([P, N // PER_COLUMN], U16, name="offsets")
+        nc.sync.dma_start(offsets[:], offs)
+
+        rows = held.tile([P, P], F32, name="rows")
+        nc.vector.memset(rows[:], 0.0)
+        for v, vector in enumerate((b, wa_z, wa_s)):
+            nc.sync.dma_start(
+                rows[v * BLOCKS : (v + 1) * BLOCKS, :],
+                vector.rearrange("(t p) o -> t (p o)", p=P),
+            )
+
+        w_sb = held.tile([K, C], BF16, name="w_sb")
+        nc.sync.dma_start(w_sb[:], w)
+        raw = [held.tile([P, S], F32, name=f"raw{t}") for t in range(BLOCKS)]
+        nc.sync.dma_start(raw[0][:], self_h[0:P, :])
+        src_sb = held.tile([K, N], BF16, name="src_sb")
+        nc.sync.dma_start(src_sb[:], src_e)
+        nc.sync.dma_start(raw[1][:], self_h[P : 2 * P, :])
+
+        identity = held.tile([P, P], F32, name="identity")
+        make_identity(nc, identity[:])
+        flipped = flip.tile([P, P], F32, name="flipped")
+        nc.tensor.transpose(flipped[:], rows[:], identity[:])
+        per_channel = held.tile([P, 3 * BLOCKS], F32, name="per_channel")
+        nc.vector.tensor_copy(per_channel[:], flipped[:, 0 : 3 * BLOCKS])
+        b_col = per_channel[:, 0:BLOCKS]
+        wa_z_col = per_channel[:, BLOCKS : 2 * BLOCKS]
+        wa_s_col = per_channel[:, 2 * BLOCKS : 3 * BLOCKS]
+        b_wa_z = held.tile([P, BLOCKS], F32, name="b_wa_z")
+        nc.vector.tensor_mul(b_wa_z[:], b_col, wa_z_col)
+
+        for t in range(BLOCKS):
+            hs = held.tile([P, S], F32, name=f"hs{t}")
+            nc.scalar.activation(hs[:], raw[t][:], IDENTITY, scale=wa_s_col[:, t : t + 1])
+
+            for first in range(0, N, PIECE):
+                zt = ring.tile([P, PIECE], F32, name="zt")
+                for lo in range(0, PIECE, BANK):
+                    bank = banks.tile([P, BANK], F32, name="bank")
+                    nc.tensor.matmul(
+                        bank[:],
+                        w_sb[:, t * P : (t + 1) * P],
+                        src_sb[:, first + lo : first + lo + BANK],
+                        start=True,
+                        stop=True,
+                    )
+                    nc.scalar.activation(
+                        zt[:, lo : lo + BANK],
+                        bank[:],
+                        IDENTITY,
+                        bias=b_wa_z[:, t : t + 1],
+                        scale=wa_z_col[:, t : t + 1],
+                    )
+
+                piece_offsets = offsets[:, first // PER_COLUMN : (first + PIECE) // PER_COLUMN]
+                total = ring.tile([P, PIECE], F32, name="total")
+                nc.vector.tensor_tensor(total[:], hs[:].indirect(piece_offsets), zt[:], ADD)
+                nc.sync.dma_start(out[t * P : (t + 1) * P, first : first + PIECE], total[:])

@@ -6,12 +6,13 @@ K, C, S, N = 128, 256, 2048, 3072
 BLOCKS = C // P
 PIECE = 1024
 BANK = 512
+CHUNK = 512
 PER_COLUMN = 16
 
 FLOPS = 2 * K * C * N
 
 F32, BF16, U16 = mybir.dt.float32, mybir.dt.bfloat16, mybir.dt.uint16
-ADD = mybir.AluOpType.add
+ADD, MULT = mybir.AluOpType.add, mybir.AluOpType.mult
 IDENTITY = mybir.ActivationFunctionType.Identity
 
 
@@ -25,22 +26,24 @@ def tile_reledgeupdate_kernel(tc, self_h, src_e, w, b, wa_z, wa_s, offs, out):
     ):
         offsets = held.tile([P, N // PER_COLUMN], U16, name="offsets")
         nc.sync.dma_start(offsets[:], offs)
+        w_sb = held.tile([K, C], BF16, name="w_sb")
+        nc.sync.dma_start(w_sb[:], w)
+        src_sb = held.tile([K, N], BF16, name="src_sb")
+        raw = [held.tile([P, S], F32, name=f"raw{t}") for t in range(BLOCKS)]
+        nc.sync.dma_start(src_sb[:, 0:PIECE], src_e[:, 0:PIECE])
+        for lo in range(0, S, CHUNK):
+            nc.sync.dma_start(raw[0][:, lo : lo + CHUNK], self_h[0:P, lo : lo + CHUNK])
+        nc.sync.dma_start(src_sb[:, PIECE:N], src_e[:, PIECE:N])
+        for lo in range(0, S, CHUNK):
+            nc.sync.dma_start(raw[1][:, lo : lo + CHUNK], self_h[P : 2 * P, lo : lo + CHUNK])
 
         rows = held.tile([P, P], F32, name="rows")
-        nc.vector.memset(rows[:], 0.0)
+        nc.gpsimd.memset(rows[:], 0.0)
         for v, vector in enumerate((b, wa_z, wa_s)):
-            nc.sync.dma_start(
+            nc.scalar.dma_start(
                 rows[v * BLOCKS : (v + 1) * BLOCKS, :],
                 vector.rearrange("(t p) o -> t (p o)", p=P),
             )
-
-        w_sb = held.tile([K, C], BF16, name="w_sb")
-        nc.sync.dma_start(w_sb[:], w)
-        raw = [held.tile([P, S], F32, name=f"raw{t}") for t in range(BLOCKS)]
-        nc.sync.dma_start(raw[0][:], self_h[0:P, :])
-        src_sb = held.tile([K, N], BF16, name="src_sb")
-        nc.sync.dma_start(src_sb[:], src_e)
-        nc.sync.dma_start(raw[1][:], self_h[P : 2 * P, :])
 
         identity = held.tile([P, P], F32, name="identity")
         make_identity(nc, identity[:])
@@ -56,7 +59,15 @@ def tile_reledgeupdate_kernel(tc, self_h, src_e, w, b, wa_z, wa_s, offs, out):
 
         for t in range(BLOCKS):
             hs = held.tile([P, S], F32, name=f"hs{t}")
-            nc.scalar.activation(hs[:], raw[t][:], IDENTITY, scale=wa_s_col[:, t : t + 1])
+            for lo in range(0, S, CHUNK):
+                if t == 0:
+                    nc.vector.tensor_scalar(
+                        hs[:, lo : lo + CHUNK], raw[t][:, lo : lo + CHUNK], wa_s_col[:, t : t + 1], None, MULT
+                    )
+                else:
+                    nc.scalar.activation(
+                        hs[:, lo : lo + CHUNK], raw[t][:, lo : lo + CHUNK], IDENTITY, scale=wa_s_col[:, t : t + 1]
+                    )
 
             for first in range(0, N, PIECE):
                 zt = ring.tile([P, PIECE], F32, name="zt")

@@ -7,7 +7,9 @@ BLOCKS = C // P
 PIECE = 1024
 BANK = 512
 CHUNK = 512
+SHORT = 256
 PER_COLUMN = 16
+ROWS = 3 * BLOCKS
 
 FLOPS = 2 * K * C * N
 
@@ -24,6 +26,12 @@ def tile_reledgeupdate_kernel(tc, self_h, src_e, w, b, wa_z, wa_s, offs, out):
         tc.psum_pool(name="flip", bufs=1) as flip,
         tc.psum_pool(name="banks", bufs=4) as banks,
     ):
+        rows = held.tile([ROWS, P], F32, name="rows")
+        for v, vector in enumerate((b, wa_z, wa_s)):
+            nc.sync.dma_start(
+                rows[v * BLOCKS : (v + 1) * BLOCKS, :],
+                vector.rearrange("(t p) o -> t (p o)", p=P),
+            )
         offsets = held.tile([P, N // PER_COLUMN], U16, name="offsets")
         nc.sync.dma_start(offsets[:], offs)
         w_sb = held.tile([K, C], BF16, name="w_sb")
@@ -37,25 +45,20 @@ def tile_reledgeupdate_kernel(tc, self_h, src_e, w, b, wa_z, wa_s, offs, out):
         for lo in range(0, S, CHUNK):
             nc.sync.dma_start(raw[1][:, lo : lo + CHUNK], self_h[P : 2 * P, lo : lo + CHUNK])
 
-        rows = held.tile([P, P], F32, name="rows")
-        nc.gpsimd.memset(rows[:], 0.0)
-        for v, vector in enumerate((b, wa_z, wa_s)):
-            nc.scalar.dma_start(
-                rows[v * BLOCKS : (v + 1) * BLOCKS, :],
-                vector.rearrange("(t p) o -> t (p o)", p=P),
-            )
-
-        identity = held.tile([P, P], F32, name="identity")
+        identity = held.tile([ROWS, ROWS], F32, name="identity")
         make_identity(nc, identity[:])
-        flipped = flip.tile([P, P], F32, name="flipped")
-        nc.tensor.transpose(flipped[:], rows[:], identity[:])
-        per_channel = held.tile([P, 3 * BLOCKS], F32, name="per_channel")
-        nc.vector.tensor_copy(per_channel[:], flipped[:, 0 : 3 * BLOCKS])
+        flipped = flip.tile([P, ROWS], F32, name="flipped")
+        nc.tensor.matmul(flipped[:], rows[:], identity[:], start=True, stop=True)
+        per_channel = held.tile([P, ROWS], F32, name="per_channel")
+        nc.vector.tensor_copy(per_channel[:], flipped[:])
         b_col = per_channel[:, 0:BLOCKS]
         wa_z_col = per_channel[:, BLOCKS : 2 * BLOCKS]
         wa_s_col = per_channel[:, 2 * BLOCKS : 3 * BLOCKS]
         b_wa_z = held.tile([P, BLOCKS], F32, name="b_wa_z")
         nc.vector.tensor_mul(b_wa_z[:], b_col, wa_z_col)
+
+        pieces = [(first, PIECE) for first in range(0, N, PIECE)]
+        pieces_of = [pieces] * (BLOCKS - 1) + [pieces[:-1] + [(N - PIECE, PIECE - SHORT), (N - SHORT, SHORT)]]
 
         for t in range(BLOCKS):
             hs = held.tile([P, S], F32, name=f"hs{t}")
@@ -69,26 +72,27 @@ def tile_reledgeupdate_kernel(tc, self_h, src_e, w, b, wa_z, wa_s, offs, out):
                         hs[:, lo : lo + CHUNK], raw[t][:, lo : lo + CHUNK], IDENTITY, scale=wa_s_col[:, t : t + 1]
                     )
 
-            for first in range(0, N, PIECE):
+            for first, size in pieces_of[t]:
                 zt = ring.tile([P, PIECE], F32, name="zt")
-                for lo in range(0, PIECE, BANK):
+                for lo in range(0, size, BANK):
+                    width = min(BANK, size - lo)
                     bank = banks.tile([P, BANK], F32, name="bank")
                     nc.tensor.matmul(
-                        bank[:],
+                        bank[:, 0:width],
                         w_sb[:, t * P : (t + 1) * P],
-                        src_sb[:, first + lo : first + lo + BANK],
+                        src_sb[:, first + lo : first + lo + width],
                         start=True,
                         stop=True,
                     )
                     nc.scalar.activation(
-                        zt[:, lo : lo + BANK],
-                        bank[:],
+                        zt[:, lo : lo + width],
+                        bank[:, 0:width],
                         IDENTITY,
                         bias=b_wa_z[:, t : t + 1],
                         scale=wa_z_col[:, t : t + 1],
                     )
 
-                piece_offsets = offsets[:, first // PER_COLUMN : (first + PIECE) // PER_COLUMN]
+                piece_offsets = offsets[:, first // PER_COLUMN : (first + size) // PER_COLUMN]
                 total = ring.tile([P, PIECE], F32, name="total")
-                nc.vector.tensor_tensor(total[:], hs[:].indirect(piece_offsets), zt[:], ADD)
-                nc.sync.dma_start(out[t * P : (t + 1) * P, first : first + PIECE], total[:])
+                nc.vector.tensor_tensor(total[:, 0:size], hs[:].indirect(piece_offsets), zt[:, 0:size], ADD)
+                nc.sync.dma_start(out[t * P : (t + 1) * P, first : first + size], total[:, 0:size])

@@ -6,7 +6,7 @@ K, C, S, N = 128, 256, 2048, 3072
 BLOCKS = C // P
 PIECE = 1024
 BANK = 512
-CHUNK = 512
+CHUNK = 1024
 SHORT = 256
 PER_COLUMN = 16
 ROWS = 3 * BLOCKS
@@ -23,8 +23,6 @@ def tile_reledgeupdate_kernel(tc, self_h, src_e, w, b, wa_z, wa_s, offs, out):
     with (
         tc.tile_pool(name="held", bufs=1) as held,
         tc.tile_pool(name="ring", bufs=3) as ring,
-        tc.psum_pool(name="flip", bufs=1) as flip,
-        tc.psum_pool(name="banks", bufs=4) as banks,
     ):
         rows = held.tile([ROWS, P], F32, name="rows")
         for v, vector in enumerate((b, wa_z, wa_s)):
@@ -47,10 +45,13 @@ def tile_reledgeupdate_kernel(tc, self_h, src_e, w, b, wa_z, wa_s, offs, out):
 
         identity = held.tile([ROWS, ROWS], F32, name="identity")
         make_identity(nc, identity[:])
-        flipped = flip.tile([P, ROWS], F32, name="flipped")
-        nc.tensor.matmul(flipped[:], rows[:], identity[:], start=True, stop=True)
+        scratch = held.tile([ROWS, ROWS], F32, name="scratch")
+        nc.scalar.activation(scratch[:], identity[:], IDENTITY)
         per_channel = held.tile([P, ROWS], F32, name="per_channel")
-        nc.vector.tensor_copy(per_channel[:], flipped[:])
+        with tc.psum_pool(name="flip", bufs=1) as flip:
+            flipped = flip.tile([P, ROWS], F32, name="flipped")
+            nc.tensor.matmul(flipped[:], rows[:], identity[:], start=True, stop=True)
+            nc.vector.tensor_copy(per_channel[:], flipped[:])
         b_col = per_channel[:, 0:BLOCKS]
         wa_z_col = per_channel[:, BLOCKS : 2 * BLOCKS]
         wa_s_col = per_channel[:, 2 * BLOCKS : 3 * BLOCKS]
@@ -60,39 +61,40 @@ def tile_reledgeupdate_kernel(tc, self_h, src_e, w, b, wa_z, wa_s, offs, out):
         pieces = [(first, PIECE) for first in range(0, N, PIECE)]
         pieces_of = [pieces] * (BLOCKS - 1) + [pieces[:-1] + [(N - PIECE, PIECE - SHORT), (N - SHORT, SHORT)]]
 
-        for t in range(BLOCKS):
-            hs = held.tile([P, S], F32, name=f"hs{t}")
-            for lo in range(0, S, CHUNK):
-                if t == 0:
-                    nc.vector.tensor_scalar(
-                        hs[:, lo : lo + CHUNK], raw[t][:, lo : lo + CHUNK], wa_s_col[:, t : t + 1], None, MULT
-                    )
-                else:
-                    nc.scalar.activation(
-                        hs[:, lo : lo + CHUNK], raw[t][:, lo : lo + CHUNK], IDENTITY, scale=wa_s_col[:, t : t + 1]
-                    )
+        with tc.psum_pool(name="banks", bufs=4) as banks:
+            for t in range(BLOCKS):
+                hs = held.tile([P, S], F32, name=f"hs{t}")
+                for lo in range(0, S, CHUNK):
+                    if t == 0:
+                        nc.vector.tensor_scalar(
+                            hs[:, lo : lo + CHUNK], raw[t][:, lo : lo + CHUNK], wa_s_col[:, t : t + 1], None, MULT
+                        )
+                    else:
+                        nc.scalar.activation(
+                            hs[:, lo : lo + CHUNK], raw[t][:, lo : lo + CHUNK], IDENTITY, scale=wa_s_col[:, t : t + 1]
+                        )
 
-            for first, size in pieces_of[t]:
-                zt = ring.tile([P, PIECE], F32, name="zt")
-                for lo in range(0, size, BANK):
-                    width = min(BANK, size - lo)
-                    bank = banks.tile([P, BANK], F32, name="bank")
-                    nc.tensor.matmul(
-                        bank[:, 0:width],
-                        w_sb[:, t * P : (t + 1) * P],
-                        src_sb[:, first + lo : first + lo + width],
-                        start=True,
-                        stop=True,
-                    )
-                    nc.scalar.activation(
-                        zt[:, lo : lo + width],
-                        bank[:, 0:width],
-                        IDENTITY,
-                        bias=b_wa_z[:, t : t + 1],
-                        scale=wa_z_col[:, t : t + 1],
-                    )
+                for first, size in pieces_of[t]:
+                    zt = ring.tile([P, PIECE], F32, name="zt")
+                    for lo in range(0, size, BANK):
+                        width = min(BANK, size - lo)
+                        bank = banks.tile([P, BANK], F32, name="bank")
+                        nc.tensor.matmul(
+                            bank[:, 0:width],
+                            w_sb[:, t * P : (t + 1) * P],
+                            src_sb[:, first + lo : first + lo + width],
+                            start=True,
+                            stop=True,
+                        )
+                        nc.scalar.activation(
+                            zt[:, lo : lo + width],
+                            bank[:, 0:width],
+                            IDENTITY,
+                            bias=b_wa_z[:, t : t + 1],
+                            scale=wa_z_col[:, t : t + 1],
+                        )
 
-                piece_offsets = offsets[:, first // PER_COLUMN : (first + size) // PER_COLUMN]
-                total = ring.tile([P, PIECE], F32, name="total")
-                nc.vector.tensor_tensor(total[:, 0:size], hs[:].indirect(piece_offsets), zt[:, 0:size], ADD)
-                nc.sync.dma_start(out[t * P : (t + 1) * P, first : first + size], total[:, 0:size])
+                    piece_offsets = offsets[:, first // PER_COLUMN : (first + size) // PER_COLUMN]
+                    total = ring.tile([P, PIECE], F32, name="total")
+                    nc.vector.tensor_tensor(total[:, 0:size], hs[:].indirect(piece_offsets), zt[:, 0:size], ADD)
+                    nc.sync.dma_start(out[t * P : (t + 1) * P, first : first + size], total[:, 0:size])

@@ -6,7 +6,7 @@ K, C, S, N = 128, 256, 2048, 3072
 BLOCKS = C // P
 PIECE = 1024
 BANK = 512
-CHUNK = 1024
+CHUNK = 512
 SHORT = 256
 PER_COLUMN = 16
 ROWS = 3 * BLOCKS

@@ -4,18 +4,18 @@ from concourse.masks import make_identity
 P = 128
 K, C, S, N = 128, 256, 2048, 3072
 BLOCKS = C // P
+ROWS = 3 * BLOCKS
+PER_COLUMN = 16
 PIECE = 1024
+SHORT = 256
 BANK = 512
 CHUNK = 512
-SHORT = 256
-PER_COLUMN = 16
-ROWS = 3 * BLOCKS
 
 FLOPS = 2 * K * C * N
 
 F32, BF16, U16 = mybir.dt.float32, mybir.dt.bfloat16, mybir.dt.uint16
 ADD, MULT = mybir.AluOpType.add, mybir.AluOpType.mult
-IDENTITY = mybir.ActivationFunctionType.Identity
+LINEAR = mybir.ActivationFunctionType.Identity
 
 
 def tile_reledgeupdate_kernel(tc, self_h, src_e, w, b, wa_z, wa_s, offs, out):
@@ -25,28 +25,30 @@ def tile_reledgeupdate_kernel(tc, self_h, src_e, w, b, wa_z, wa_s, offs, out):
         tc.tile_pool(name="ring", bufs=3) as ring,
     ):
         rows = held.tile([ROWS, P], F32, name="rows")
-        for v, vector in enumerate((b, wa_z, wa_s)):
+        for v, param in enumerate((b, wa_z, wa_s)):
             nc.sync.dma_start(
                 rows[v * BLOCKS : (v + 1) * BLOCKS, :],
-                vector.rearrange("(t p) o -> t (p o)", p=P),
+                param.rearrange("(t p) o -> t (p o)", p=P),
             )
-        offsets = held.tile([P, N // PER_COLUMN], U16, name="offsets")
-        nc.sync.dma_start(offsets[:], offs)
         w_sb = held.tile([K, C], BF16, name="w_sb")
         nc.sync.dma_start(w_sb[:], w)
         src_sb = held.tile([K, N], BF16, name="src_sb")
-        raw = [held.tile([P, S], F32, name=f"raw{t}") for t in range(BLOCKS)]
         nc.sync.dma_start(src_sb[:, 0:PIECE], src_e[:, 0:PIECE])
-        for lo in range(0, S, CHUNK):
-            nc.sync.dma_start(raw[0][:, lo : lo + CHUNK], self_h[0:P, lo : lo + CHUNK])
+        raw = [held.tile([P, S], F32, name=f"raw{t}") for t in range(BLOCKS)]
+        for node in range(0, S, CHUNK):
+            nc.sync.dma_start(raw[0][:, node : node + CHUNK], self_h[0:P, node : node + CHUNK])
+        offsets = held.tile([P, N // PER_COLUMN], U16, name="offsets")
+        nc.sync.dma_start(offsets[:], offs)
         nc.sync.dma_start(src_sb[:, PIECE:N], src_e[:, PIECE:N])
-        for lo in range(0, S, CHUNK):
-            nc.sync.dma_start(raw[1][:, lo : lo + CHUNK], self_h[P : 2 * P, lo : lo + CHUNK])
+        for node in range(0, S, CHUNK):
+            nc.sync.dma_start(
+                raw[1][:, node : node + CHUNK], self_h[P : 2 * P, node : node + CHUNK]
+            )
 
         identity = held.tile([ROWS, ROWS], F32, name="identity")
         make_identity(nc, identity[:])
         scratch = held.tile([ROWS, ROWS], F32, name="scratch")
-        nc.scalar.activation(scratch[:], identity[:], IDENTITY)
+        nc.scalar.activation(scratch[:], identity[:], LINEAR)
         per_channel = held.tile([P, ROWS], F32, name="per_channel")
         with tc.psum_pool(name="flip", bufs=1) as flip:
             flipped = flip.tile([P, ROWS], F32, name="flipped")
@@ -59,42 +61,54 @@ def tile_reledgeupdate_kernel(tc, self_h, src_e, w, b, wa_z, wa_s, offs, out):
         nc.vector.tensor_mul(b_wa_z[:], b_col, wa_z_col)
 
         pieces = [(first, PIECE) for first in range(0, N, PIECE)]
-        pieces_of = [pieces] * (BLOCKS - 1) + [pieces[:-1] + [(N - PIECE, PIECE - SHORT), (N - SHORT, SHORT)]]
+        recut = pieces[:-1] + [(N - PIECE, PIECE - SHORT), (N - SHORT, SHORT)]
+        pieces_of = [pieces, recut]
 
         with tc.psum_pool(name="banks", bufs=4) as banks:
             for t in range(BLOCKS):
                 hs = held.tile([P, S], F32, name=f"hs{t}")
-                for lo in range(0, S, CHUNK):
+                for node in range(0, S, CHUNK):
                     if t == 0:
                         nc.vector.tensor_scalar(
-                            hs[:, lo : lo + CHUNK], raw[t][:, lo : lo + CHUNK], wa_s_col[:, t : t + 1], None, MULT
+                            hs[:, node : node + CHUNK],
+                            raw[t][:, node : node + CHUNK],
+                            wa_s_col[:, t : t + 1],
+                            None,
+                            MULT,
                         )
                     else:
                         nc.scalar.activation(
-                            hs[:, lo : lo + CHUNK], raw[t][:, lo : lo + CHUNK], IDENTITY, scale=wa_s_col[:, t : t + 1]
+                            hs[:, node : node + CHUNK],
+                            raw[t][:, node : node + CHUNK],
+                            LINEAR,
+                            scale=wa_s_col[:, t : t + 1],
                         )
 
                 for first, size in pieces_of[t]:
                     zt = ring.tile([P, PIECE], F32, name="zt")
-                    for lo in range(0, size, BANK):
-                        width = min(BANK, size - lo)
+                    for col in range(0, size, BANK):
+                        width = min(BANK, size - col)
                         bank = banks.tile([P, BANK], F32, name="bank")
                         nc.tensor.matmul(
                             bank[:, 0:width],
                             w_sb[:, t * P : (t + 1) * P],
-                            src_sb[:, first + lo : first + lo + width],
+                            src_sb[:, first + col : first + col + width],
                             start=True,
                             stop=True,
                         )
                         nc.scalar.activation(
-                            zt[:, lo : lo + width],
+                            zt[:, col : col + width],
                             bank[:, 0:width],
-                            IDENTITY,
+                            LINEAR,
                             bias=b_wa_z[:, t : t + 1],
                             scale=wa_z_col[:, t : t + 1],
                         )
 
                     piece_offsets = offsets[:, first // PER_COLUMN : (first + size) // PER_COLUMN]
                     total = ring.tile([P, PIECE], F32, name="total")
-                    nc.vector.tensor_tensor(total[:, 0:size], hs[:].indirect(piece_offsets), zt[:, 0:size], ADD)
-                    nc.sync.dma_start(out[t * P : (t + 1) * P, first : first + size], total[:, 0:size])
+                    nc.vector.tensor_tensor(
+                        total[:, 0:size], hs[:].indirect(piece_offsets), zt[:, 0:size], ADD
+                    )
+                    nc.sync.dma_start(
+                        out[t * P : (t + 1) * P, first : first + size], total[:, 0:size]
+                    )

@@ -30,15 +30,15 @@ def tile_reledgeupdate_kernel(tc, self_h, src_e, w, b, wa_z, wa_s, offs, out):
                 rows[v * BLOCKS : (v + 1) * BLOCKS, :],
                 param.rearrange("(t p) o -> t (p o)", p=P),
             )
+        offsets = held.tile([P, N // PER_COLUMN], U16, name="offsets")
+        nc.sync.dma_start(offsets[:], offs)
         w_sb = held.tile([K, C], BF16, name="w_sb")
         nc.sync.dma_start(w_sb[:], w)
         src_sb = held.tile([K, N], BF16, name="src_sb")
-        nc.sync.dma_start(src_sb[:, 0:PIECE], src_e[:, 0:PIECE])
         raw = [held.tile([P, S], F32, name=f"raw{t}") for t in range(BLOCKS)]
+        nc.sync.dma_start(src_sb[:, 0:PIECE], src_e[:, 0:PIECE])
         for node in range(0, S, CHUNK):
             nc.sync.dma_start(raw[0][:, node : node + CHUNK], self_h[0:P, node : node + CHUNK])
-        offsets = held.tile([P, N // PER_COLUMN], U16, name="offsets")
-        nc.sync.dma_start(offsets[:], offs)
         nc.sync.dma_start(src_sb[:, PIECE:N], src_e[:, PIECE:N])
         for node in range(0, S, CHUNK):
             nc.sync.dma_start(

@@ -7,7 +7,7 @@ BLOCKS = C // P
 ROWS = 3 * BLOCKS
 PER_COLUMN = 16
 PIECE = 1024
-SHORT = 256
+TAPER = (512, 256, 128, 128)
 BANK = 512
 CHUNK = 512
 
@@ -20,10 +20,7 @@ LINEAR = mybir.ActivationFunctionType.Identity
 
 def tile_reledgeupdate_kernel(tc, self_h, src_e, w, b, wa_z, wa_s, offs, out):
     nc = tc.nc
-    with (
-        tc.tile_pool(name="held", bufs=1) as held,
-        tc.tile_pool(name="ring", bufs=3) as ring,
-    ):
+    with tc.tile_pool(name="held", bufs=1) as held:
         rows = held.tile([ROWS, P], F32, name="rows")
         for v, param in enumerate((b, wa_z, wa_s)):
             nc.sync.dma_start(
@@ -61,7 +58,9 @@ def tile_reledgeupdate_kernel(tc, self_h, src_e, w, b, wa_z, wa_s, offs, out):
         nc.vector.tensor_mul(b_wa_z[:], b_col, wa_z_col)
 
         pieces = [(first, PIECE) for first in range(0, N, PIECE)]
-        recut = pieces[:-1] + [(N - PIECE, PIECE - SHORT), (N - SHORT, SHORT)]
+        recut = pieces[:-1] + [
+            (N - PIECE + sum(TAPER[:i]), size) for i, size in enumerate(TAPER)
+        ]
         pieces_of = [pieces, recut]
 
         with tc.psum_pool(name="banks", bufs=4) as banks:
@@ -84,31 +83,34 @@ def tile_reledgeupdate_kernel(tc, self_h, src_e, w, b, wa_z, wa_s, offs, out):
                             scale=wa_s_col[:, t : t + 1],
                         )
 
-                for first, size in pieces_of[t]:
-                    zt = ring.tile([P, PIECE], F32, name="zt")
-                    for col in range(0, size, BANK):
-                        width = min(BANK, size - col)
-                        bank = banks.tile([P, BANK], F32, name="bank")
-                        nc.tensor.matmul(
-                            bank[:, 0:width],
-                            w_sb[:, t * P : (t + 1) * P],
-                            src_sb[:, first + col : first + col + width],
-                            start=True,
-                            stop=True,
-                        )
-                        nc.scalar.activation(
-                            zt[:, col : col + width],
-                            bank[:, 0:width],
-                            LINEAR,
-                            bias=b_wa_z[:, t : t + 1],
-                            scale=wa_z_col[:, t : t + 1],
-                        )
+                zt = held.tile([P, N], F32, name=f"zt{t}")
+                for edge in range(0, N, BANK):
+                    bank = banks.tile([P, BANK], F32, name="bank")
+                    nc.tensor.matmul(
+                        bank[:],
+                        w_sb[:, t * P : (t + 1) * P],
+                        src_sb[:, edge : edge + BANK],
+                        start=True,
+                        stop=True,
+                    )
+                    nc.scalar.activation(
+                        zt[:, edge : edge + BANK],
+                        bank[:],
+                        LINEAR,
+                        bias=b_wa_z[:, t : t + 1],
+                        scale=wa_z_col[:, t : t + 1],
+                    )
 
+                total = held.tile([P, N], F32, name=f"total{t}")
+                for first, size in pieces_of[t]:
                     piece_offsets = offsets[:, first // PER_COLUMN : (first + size) // PER_COLUMN]
-                    total = ring.tile([P, PIECE], F32, name="total")
                     nc.vector.tensor_tensor(
-                        total[:, 0:size], hs[:].indirect(piece_offsets), zt[:, 0:size], ADD
+                        total[:, first : first + size],
+                        hs[:].indirect(piece_offsets),
+                        zt[:, first : first + size],
+                        ADD,
                     )
                     nc.sync.dma_start(
-                        out[t * P : (t + 1) * P, first : first + size], total[:, 0:size]
+                        out[t * P : (t + 1) * P, first : first + size],
+                        total[:, first : first + size],
                     )

@@ -7,6 +7,7 @@ BLOCKS = C // P
 ROWS = 3 * BLOCKS
 PER_COLUMN = 16
 PIECE = 1024
+FIRST = 512
 TAPER = (512, 256, 128, 128)
 BANK = 512
 CHUNK = 512
@@ -29,14 +30,21 @@ def tile_reledgeupdate_kernel(tc, self_h, src_e, w, b, wa_z, wa_s, offs, out):
             )
         offsets = held.tile([P, N // PER_COLUMN], U16, name="offsets")
         nc.sync.dma_start(offsets[:], offs)
+        pieces = [(first, PIECE) for first in range(0, N, PIECE)]
+        pieces_of = [
+            [(0, FIRST), (FIRST, PIECE - FIRST)] + pieces[1:],
+            pieces[:-1]
+            + [(N - PIECE + sum(TAPER[:i]), size) for i, size in enumerate(TAPER)],
+        ]
         w_sb = held.tile([K, C], BF16, name="w_sb")
         nc.sync.dma_start(w_sb[:], w)
         src_sb = held.tile([K, N], BF16, name="src_sb")
         raw = [held.tile([P, S], F32, name=f"raw{t}") for t in range(BLOCKS)]
-        nc.sync.dma_start(src_sb[:, 0:PIECE], src_e[:, 0:PIECE])
+        nc.sync.dma_start(src_sb[:, 0:FIRST], src_e[:, 0:FIRST])
         for node in range(0, S, CHUNK):
             nc.sync.dma_start(raw[0][:, node : node + CHUNK], self_h[0:P, node : node + CHUNK])
-        nc.sync.dma_start(src_sb[:, PIECE:N], src_e[:, PIECE:N])
+        for first, size in pieces_of[0][1:]:
+            nc.sync.dma_start(src_sb[:, first : first + size], src_e[:, first : first + size])
         for node in range(0, S, CHUNK):
             nc.sync.dma_start(
                 raw[1][:, node : node + CHUNK], self_h[P : 2 * P, node : node + CHUNK]
@@ -56,12 +64,6 @@ def tile_reledgeupdate_kernel(tc, self_h, src_e, w, b, wa_z, wa_s, offs, out):
         wa_s_col = per_channel[:, 2 * BLOCKS : 3 * BLOCKS]
         b_wa_z = held.tile([P, BLOCKS], F32, name="b_wa_z")
         nc.vector.tensor_mul(b_wa_z[:], b_col, wa_z_col)
-
-        pieces = [(first, PIECE) for first in range(0, N, PIECE)]
-        recut = pieces[:-1] + [
-            (N - PIECE + sum(TAPER[:i]), size) for i, size in enumerate(TAPER)
-        ]
-        pieces_of = [pieces, recut]
 
         with tc.psum_pool(name="banks", bufs=4) as banks:
             for t in range(BLOCKS):

@@ -7,7 +7,7 @@ BLOCKS = C // P
 ROWS = 3 * BLOCKS
 PER_COLUMN = 16
 PIECE = 1024
-FIRST = 512
+HEAD = (256, 256, 512)
 TAPER = (512, 256, 128, 128)
 BANK = 512
 CHUNK = 512
@@ -32,7 +32,7 @@ def tile_reledgeupdate_kernel(tc, self_h, src_e, w, b, wa_z, wa_s, offs, out):
         nc.sync.dma_start(offsets[:], offs)
         pieces = [(first, PIECE) for first in range(0, N, PIECE)]
         pieces_of = [
-            [(0, FIRST), (FIRST, PIECE - FIRST)] + pieces[1:],
+            [(sum(HEAD[:i]), size) for i, size in enumerate(HEAD)] + pieces[1:],
             pieces[:-1]
             + [(N - PIECE + sum(TAPER[:i]), size) for i, size in enumerate(TAPER)],
         ]
@@ -40,7 +40,7 @@ def tile_reledgeupdate_kernel(tc, self_h, src_e, w, b, wa_z, wa_s, offs, out):
         nc.sync.dma_start(w_sb[:], w)
         src_sb = held.tile([K, N], BF16, name="src_sb")
         raw = [held.tile([P, S], F32, name=f"raw{t}") for t in range(BLOCKS)]
-        nc.sync.dma_start(src_sb[:, 0:FIRST], src_e[:, 0:FIRST])
+        nc.sync.dma_start(src_sb[:, 0 : HEAD[0]], src_e[:, 0 : HEAD[0]])
         for node in range(0, S, CHUNK):
             nc.sync.dma_start(raw[0][:, node : node + CHUNK], self_h[0:P, node : node + CHUNK])
         for first, size in pieces_of[0][1:]:
@@ -86,18 +86,23 @@ def tile_reledgeupdate_kernel(tc, self_h, src_e, w, b, wa_z, wa_s, offs, out):
                         )
 
                 zt = held.tile([P, N], F32, name=f"zt{t}")
-                for edge in range(0, N, BANK):
+                widths = [
+                    (first + col, min(BANK, size - col))
+                    for first, size in pieces_of[0]
+                    for col in range(0, size, BANK)
+                ]
+                for edge, width in widths:
                     bank = banks.tile([P, BANK], F32, name="bank")
                     nc.tensor.matmul(
-                        bank[:],
+                        bank[:, 0:width],
                         w_sb[:, t * P : (t + 1) * P],
-                        src_sb[:, edge : edge + BANK],
+                        src_sb[:, edge : edge + width],
                         start=True,
                         stop=True,
                     )
                     nc.scalar.activation(
-                        zt[:, edge : edge + BANK],
-                        bank[:],
+                        zt[:, edge : edge + width],
+                        bank[:, 0:width],
                         LINEAR,
                         bias=b_wa_z[:, t : t + 1],
                         scale=wa_z_col[:, t : t + 1],

@@ -52,8 +52,6 @@ def tile_reledgeupdate_kernel(tc, self_h, src_e, w, b, wa_z, wa_s, offs, out):
 
         identity = held.tile([ROWS, ROWS], F32, name="identity")
         make_identity(nc, identity[:])
-        scratch = held.tile([ROWS, ROWS], F32, name="scratch")
-        nc.scalar.activation(scratch[:], identity[:], LINEAR)
         per_channel = held.tile([P, ROWS], F32, name="per_channel")
         with tc.psum_pool(name="flip", bufs=1) as flip:
             flipped = flip.tile([P, ROWS], F32, name="flipped")

@@ -10,7 +10,7 @@ PIECE = 1024
 HEAD = (256, 256, 512)
 TAPER = (512, 256, 128, 128)
 BANK = 512
-CHUNK = 512
+CHUNKS = (1152, 576, 320)
 
 FLOPS = 2 * K * C * N
 
@@ -29,7 +29,6 @@ def tile_reledgeupdate_kernel(tc, self_h, src_e, w, b, wa_z, wa_s, offs, out):
                 param.rearrange("(t p) o -> t (p o)", p=P),
             )
         offsets = held.tile([P, N // PER_COLUMN], U16, name="offsets")
-        nc.sync.dma_start(offsets[:], offs)
         pieces = [(first, PIECE) for first in range(0, N, PIECE)]
         pieces_of = [
             [(sum(HEAD[:i]), size) for i, size in enumerate(HEAD)] + pieces[1:],
@@ -39,19 +38,21 @@ def tile_reledgeupdate_kernel(tc, self_h, src_e, w, b, wa_z, wa_s, offs, out):
         w_sb = held.tile([K, C], BF16, name="w_sb")
         nc.sync.dma_start(w_sb[:], w)
         src_sb = held.tile([K, N], BF16, name="src_sb")
+        chunks = [(sum(CHUNKS[:i]), size) for i, size in enumerate(CHUNKS)]
         raw = [held.tile([P, S], F32, name=f"raw{t}") for t in range(BLOCKS)]
         nc.sync.dma_start(src_sb[:, 0 : HEAD[0]], src_e[:, 0 : HEAD[0]])
-        for node in range(0, S, CHUNK):
-            nc.sync.dma_start(raw[0][:, node : node + CHUNK], self_h[0:P, node : node + CHUNK])
+        for node, size in chunks:
+            nc.sync.dma_start(raw[0][:, node : node + size], self_h[0:P, node : node + size])
+        nc.sync.dma_start(offsets[:], offs)
         for first, size in pieces_of[0][1:]:
             nc.sync.dma_start(src_sb[:, first : first + size], src_e[:, first : first + size])
-        for node in range(0, S, CHUNK):
-            nc.sync.dma_start(
-                raw[1][:, node : node + CHUNK], self_h[P : 2 * P, node : node + CHUNK]
-            )
+        for node, size in chunks:
+            nc.sync.dma_start(raw[1][:, node : node + size], self_h[P : 2 * P, node : node + size])
 
         identity = held.tile([ROWS, ROWS], F32, name="identity")
         make_identity(nc, identity[:])
+        scratch = held.tile([ROWS, ROWS], F32, name="scratch")
+        nc.scalar.activation(scratch[:], identity[:], LINEAR)
         per_channel = held.tile([P, ROWS], F32, name="per_channel")
         with tc.psum_pool(name="flip", bufs=1) as flip:
             flipped = flip.tile([P, ROWS], F32, name="flipped")
@@ -66,19 +67,19 @@ def tile_reledgeupdate_kernel(tc, self_h, src_e, w, b, wa_z, wa_s, offs, out):
         with tc.psum_pool(name="banks", bufs=4) as banks:
             for t in range(BLOCKS):
                 hs = held.tile([P, S], F32, name=f"hs{t}")
-                for node in range(0, S, CHUNK):
+                for node, size in chunks:
                     if t == 0:
                         nc.vector.tensor_scalar(
-                            hs[:, node : node + CHUNK],
-                            raw[t][:, node : node + CHUNK],
+                            hs[:, node : node + size],
+                            raw[t][:, node : node + size],
                             wa_s_col[:, t : t + 1],
                             None,
                             MULT,
                         )
                     else:
                         nc.scalar.activation(
-                            hs[:, node : node + CHUNK],
-                            raw[t][:, node : node + CHUNK],
+                            hs[:, node : node + size],
+                            raw[t][:, node : node + size],
                             LINEAR,
                             scale=wa_s_col[:, t : t + 1],
                         )

@@ -7,7 +7,7 @@ BLOCKS = C // P
 ROWS = 3 * BLOCKS
 PER_COLUMN = 16
 PIECE = 1024
-HEAD = (256, 256, 512)
+HEAD = (512, 256, 256, 512, 512, 1024)
 TAPER = (512, 256, 128, 128)
 BANK = 512
 CHUNKS = (1152, 576, 320)
@@ -29,12 +29,8 @@ def tile_reledgeupdate_kernel(tc, self_h, src_e, w, b, wa_z, wa_s, offs, out):
                 param.rearrange("(t p) o -> t (p o)", p=P),
             )
         offsets = held.tile([P, N // PER_COLUMN], U16, name="offsets")
-        pieces = [(first, PIECE) for first in range(0, N, PIECE)]
-        pieces_of = [
-            [(sum(HEAD[:i]), size) for i, size in enumerate(HEAD)] + pieces[1:],
-            pieces[:-1]
-            + [(N - PIECE + sum(TAPER[:i]), size) for i, size in enumerate(TAPER)],
-        ]
+        sizes_of = [HEAD, (PIECE, PIECE) + TAPER]
+        pieces_of = [[(sum(sizes[:i]), size) for i, size in enumerate(sizes)] for sizes in sizes_of]
         w_sb = held.tile([K, C], BF16, name="w_sb")
         nc.sync.dma_start(w_sb[:], w)
         src_sb = held.tile([K, N], BF16, name="src_sb")
@@ -43,9 +39,10 @@ def tile_reledgeupdate_kernel(tc, self_h, src_e, w, b, wa_z, wa_s, offs, out):
         nc.sync.dma_start(src_sb[:, 0 : HEAD[0]], src_e[:, 0 : HEAD[0]])
         for node, size in chunks:
             nc.sync.dma_start(raw[0][:, node : node + size], self_h[0:P, node : node + size])
-        nc.sync.dma_start(offsets[:], offs)
-        for first, size in pieces_of[0][1:]:
+        for i, (first, size) in enumerate(pieces_of[0][1:]):
             nc.sync.dma_start(src_sb[:, first : first + size], src_e[:, first : first + size])
+            if i == 0:
+                nc.sync.dma_start(offsets[:], offs)
         for node, size in chunks:
             nc.sync.dma_start(raw[1][:, node : node + size], self_h[P : 2 * P, node : node + size])
 

@@ -7,7 +7,7 @@ BLOCKS = C // P
 ROWS = 3 * BLOCKS
 PER_COLUMN = 16
 PIECE = 1024
-HEAD = (512, 256, 256, 512, 512, 1024)
+HEAD = (384, 128, 256, 256, 512, 512, 1024)
 TAPER = (512, 256, 128, 128)
 BANK = 512
 CHUNKS = (1152, 576, 320)
@@ -39,10 +39,9 @@ def tile_reledgeupdate_kernel(tc, self_h, src_e, w, b, wa_z, wa_s, offs, out):
         nc.sync.dma_start(src_sb[:, 0 : HEAD[0]], src_e[:, 0 : HEAD[0]])
         for node, size in chunks:
             nc.sync.dma_start(raw[0][:, node : node + size], self_h[0:P, node : node + size])
-        for i, (first, size) in enumerate(pieces_of[0][1:]):
+        nc.sync.dma_start(offsets[:], offs)
+        for first, size in pieces_of[0][1:]:
             nc.sync.dma_start(src_sb[:, first : first + size], src_e[:, first : first + size])
-            if i == 0:
-                nc.sync.dma_start(offsets[:], offs)
         for node, size in chunks:
             nc.sync.dma_start(raw[1][:, node : node + size], self_h[P : 2 * P, node : node + size])
 

@@ -1,10 +1,9 @@
 import concourse.mybir as mybir
-from concourse.masks import make_identity
 
 P = 128
 K, C, S, N = 128, 256, 2048, 3072
 BLOCKS = C // P
-ROWS = 3 * BLOCKS
+TURN = 32
 PER_COLUMN = 16
 PIECE = 1024
 HEAD = (384, 128, 256, 256, 512, 512, 1024)
@@ -22,12 +21,6 @@ LINEAR = mybir.ActivationFunctionType.Identity
 def tile_reledgeupdate_kernel(tc, self_h, src_e, w, b, wa_z, wa_s, offs, out):
     nc = tc.nc
     with tc.tile_pool(name="held", bufs=1) as held:
-        rows = held.tile([ROWS, P], F32, name="rows")
-        for v, param in enumerate((b, wa_z, wa_s)):
-            nc.sync.dma_start(
-                rows[v * BLOCKS : (v + 1) * BLOCKS, :],
-                param.rearrange("(t p) o -> t (p o)", p=P),
-            )
         offsets = held.tile([P, N // PER_COLUMN], U16, name="offsets")
         sizes_of = [HEAD, (PIECE, PIECE) + TAPER]
         pieces_of = [[(sum(sizes[:i]), size) for i, size in enumerate(sizes)] for sizes in sizes_of]
@@ -37,6 +30,13 @@ def tile_reledgeupdate_kernel(tc, self_h, src_e, w, b, wa_z, wa_s, offs, out):
         chunks = [(sum(CHUNKS[:i]), size) for i, size in enumerate(CHUNKS)]
         raw = [held.tile([P, S], F32, name=f"raw{t}") for t in range(BLOCKS)]
         nc.sync.dma_start(src_sb[:, 0 : HEAD[0]], src_e[:, 0 : HEAD[0]])
+        rows = held.tile([P, BLOCKS * TURN], F32, name="rows", align_bytes=64)
+        nc.vector.memset(rows[:], 0.0)
+        by_block = rows[:].rearrange("(q r) (t j) -> q r t j", r=TURN, j=TURN)
+        for v, param in enumerate((b, wa_z, wa_s)):
+            nc.sync.dma_start(
+                by_block[:, v], param.rearrange("(t q j) o -> q t (j o)", t=BLOCKS, j=TURN)
+            )
         for node, size in chunks:
             nc.sync.dma_start(raw[0][:, node : node + size], self_h[0:P, node : node + size])
         nc.sync.dma_start(offsets[:], offs)
@@ -45,20 +45,19 @@ def tile_reledgeupdate_kernel(tc, self_h, src_e, w, b, wa_z, wa_s, offs, out):
         for node, size in chunks:
             nc.sync.dma_start(raw[1][:, node : node + size], self_h[P : 2 * P, node : node + size])
 
-        identity = held.tile([ROWS, ROWS], F32, name="identity")
-        make_identity(nc, identity[:])
-        scratch = held.tile([ROWS, ROWS], F32, name="scratch")
-        nc.scalar.activation(scratch[:], identity[:], LINEAR)
-        per_channel = held.tile([P, ROWS], F32, name="per_channel")
-        with tc.psum_pool(name="flip", bufs=1) as flip:
-            flipped = flip.tile([P, ROWS], F32, name="flipped")
-            nc.tensor.matmul(flipped[:], rows[:], identity[:], start=True, stop=True)
-            nc.vector.tensor_copy(per_channel[:], flipped[:])
-        b_col = per_channel[:, 0:BLOCKS]
-        wa_z_col = per_channel[:, BLOCKS : 2 * BLOCKS]
-        wa_s_col = per_channel[:, 2 * BLOCKS : 3 * BLOCKS]
-        b_wa_z = held.tile([P, BLOCKS], F32, name="b_wa_z")
-        nc.vector.tensor_mul(b_wa_z[:], b_col, wa_z_col)
+        scratch = held.tile([P, 2], F32, name="scratch")
+        nc.vector.memset(scratch[:, 0:1], 0.0)
+        nc.scalar.activation(scratch[:, 1:2], scratch[:, 0:1], LINEAR)
+        turned = []
+        for t in range(BLOCKS):
+            columns = held.tile([P, TURN], F32, name=f"turned{t}", align_bytes=64)
+            nc.vector.transpose(columns[:], rows[:, t * TURN : (t + 1) * TURN])
+            turned.append(columns)
+        wa_z_col = [columns[:, 1:2] for columns in turned]
+        wa_s_col = [columns[:, 2:3] for columns in turned]
+        b_wa_z = [held.tile([P, 1], F32, name=f"b_wa_z{t}") for t in range(BLOCKS)]
+        for t in range(BLOCKS):
+            nc.vector.tensor_mul(b_wa_z[t][:], turned[t][:, 0:1], wa_z_col[t])
 
         with tc.psum_pool(name="banks", bufs=4) as banks:
             for t in range(BLOCKS):
@@ -68,7 +67,7 @@ def tile_reledgeupdate_kernel(tc, self_h, src_e, w, b, wa_z, wa_s, offs, out):
                         nc.vector.tensor_scalar(
                             hs[:, node : node + size],
                             raw[t][:, node : node + size],
-                            wa_s_col[:, t : t + 1],
+                            wa_s_col[t],
                             None,
                             MULT,
                         )
@@ -77,7 +76,7 @@ def tile_reledgeupdate_kernel(tc, self_h, src_e, w, b, wa_z, wa_s, offs, out):
                             hs[:, node : node + size],
                             raw[t][:, node : node + size],
                             LINEAR,
-                            scale=wa_s_col[:, t : t + 1],
+                            scale=wa_s_col[t],
                         )
 
                 zt = held.tile([P, N], F32, name=f"zt{t}")
@@ -99,8 +98,8 @@ def tile_reledgeupdate_kernel(tc, self_h, src_e, w, b, wa_z, wa_s, offs, out):
                         zt[:, edge : edge + width],
                         bank[:, 0:width],
                         LINEAR,
-                        bias=b_wa_z[:, t : t + 1],
-                        scale=wa_z_col[:, t : t + 1],
+                        bias=b_wa_z[t][:],
+                        scale=wa_z_col[t],
                     )
 
                 total = held.tile([P, N], F32, name=f"total{t}")

@@ -25,7 +25,7 @@ def tile_reledgeupdate_kernel(tc, self_h, src_e, w, b, wa_z, wa_s, offs, out):
         sizes_of = [HEAD, (PIECE, PIECE) + TAPER]
         pieces_of = [[(sum(sizes[:i]), size) for i, size in enumerate(sizes)] for sizes in sizes_of]
         w_sb = held.tile([K, C], BF16, name="w_sb")
-        nc.sync.dma_start(w_sb[:], w)
+        nc.sync.dma_start(w_sb[:, 0:P], w[:, 0:P])
         src_sb = held.tile([K, N], BF16, name="src_sb")
         chunks = [(sum(CHUNKS[:i]), size) for i, size in enumerate(CHUNKS)]
         raw = [held.tile([P, S], F32, name=f"raw{t}") for t in range(BLOCKS)]
@@ -42,12 +42,10 @@ def tile_reledgeupdate_kernel(tc, self_h, src_e, w, b, wa_z, wa_s, offs, out):
         nc.sync.dma_start(offsets[:], offs)
         for first, size in pieces_of[0][1:]:
             nc.sync.dma_start(src_sb[:, first : first + size], src_e[:, first : first + size])
+        nc.sync.dma_start(w_sb[:, P:C], w[:, P:C])
         for node, size in chunks:
             nc.sync.dma_start(raw[1][:, node : node + size], self_h[P : 2 * P, node : node + size])
 
-        scratch = held.tile([P, 2], F32, name="scratch")
-        nc.vector.memset(scratch[:, 0:1], 0.0)
-        nc.scalar.activation(scratch[:, 1:2], scratch[:, 0:1], LINEAR)
         turned = []
         for t in range(BLOCKS):
             columns = held.tile([P, TURN], F32, name=f"turned{t}", align_bytes=64)
@@ -57,9 +55,47 @@ def tile_reledgeupdate_kernel(tc, self_h, src_e, w, b, wa_z, wa_s, offs, out):
         wa_s_col = [columns[:, 2:3] for columns in turned]
         b_wa_z = [held.tile([P, 1], F32, name=f"b_wa_z{t}") for t in range(BLOCKS)]
         for t in range(BLOCKS):
-            nc.vector.tensor_mul(b_wa_z[t][:], turned[t][:, 0:1], wa_z_col[t])
+            nc.scalar.activation(b_wa_z[t][:], turned[t][:, 0:1], LINEAR, scale=wa_z_col[t])
 
         with tc.psum_pool(name="banks", bufs=4) as banks:
+            zt = [held.tile([P, N], F32, name=f"zt{t}") for t in range(BLOCKS)]
+
+            def project(t, edge, width):
+                bank = banks.tile([P, BANK], F32, name="bank")
+                nc.tensor.matmul(
+                    bank[:, 0:width],
+                    w_sb[:, t * P : (t + 1) * P],
+                    src_sb[:, edge : edge + width],
+                    start=True,
+                    stop=True,
+                )
+                return bank
+
+            def scale_on_scalar(t, edge, width, bank):
+                nc.scalar.activation(
+                    zt[t][:, edge : edge + width],
+                    bank[:, 0:width],
+                    LINEAR,
+                    bias=b_wa_z[t][:],
+                    scale=wa_z_col[t],
+                )
+
+            widths = [
+                (first + col, min(BANK, size - col))
+                for first, size in pieces_of[0]
+                for col in range(0, size, BANK)
+            ]
+            edge, width = widths[0]
+            bank = project(0, edge, width)
+            nc.vector.tensor_scalar(
+                zt[0][:, edge : edge + width],
+                bank[:, 0:width],
+                turned[0][:, 0:1],
+                wa_z_col[0],
+                ADD,
+                MULT,
+            )
+
             for t in range(BLOCKS):
                 hs = held.tile([P, S], F32, name=f"hs{t}")
                 for node, size in chunks:
@@ -79,28 +115,8 @@ def tile_reledgeupdate_kernel(tc, self_h, src_e, w, b, wa_z, wa_s, offs, out):
                             scale=wa_s_col[t],
                         )
 
-                zt = held.tile([P, N], F32, name=f"zt{t}")
-                widths = [
-                    (first + col, min(BANK, size - col))
-                    for first, size in pieces_of[0]
-                    for col in range(0, size, BANK)
-                ]
-                for edge, width in widths:
-                    bank = banks.tile([P, BANK], F32, name="bank")
-                    nc.tensor.matmul(
-                        bank[:, 0:width],
-                        w_sb[:, t * P : (t + 1) * P],
-                        src_sb[:, edge : edge + width],
-                        start=True,
-                        stop=True,
-                    )
-                    nc.scalar.activation(
-                        zt[:, edge : edge + width],
-                        bank[:, 0:width],
-                        LINEAR,
-                        bias=b_wa_z[t][:],
-                        scale=wa_z_col[t],
-                    )
+                for edge, width in widths if t else widths[1:]:
+                    scale_on_scalar(t, edge, width, project(t, edge, width))
 
                 total = held.tile([P, N], F32, name=f"total{t}")
                 for first, size in pieces_of[t]:
@@ -108,7 +124,7 @@ def tile_reledgeupdate_kernel(tc, self_h, src_e, w, b, wa_z, wa_s, offs, out):
                     nc.vector.tensor_tensor(
                         total[:, first : first + size],
                         hs[:].indirect(piece_offsets),
-                        zt[:, first : first + size],
+                        zt[t][:, first : first + size],
                         ADD,
                     )
                     nc.sync.dma_start(

@@ -6,10 +6,10 @@ BLOCKS = C // P
 TURN = 32
 PER_COLUMN = 16
 PIECE = 1024
-HEAD = (384, 128, 256, 256, 512, 512, 1024)
+HEAD = (512, 256, 256, 512, 512, 1024)
 TAPER = (512, 256, 128, 128)
 BANK = 512
-CHUNKS = (1152, 576, 320)
+CHUNKS = (1024, 512, 256, 256)
 
 FLOPS = 2 * K * C * N
 

import concourse.mybir as mybir

P = 128
K, C, S, N = 128, 256, 2048, 3072
BLOCKS = C // P
TURN = 32
PER_COLUMN = 16
PIECE = 1024
HEAD = (512, 256, 256, 512, 512, 1024)
TAPER = (512, 256, 128, 128)
BANK = 512
CHUNKS = (1024, 512, 256, 256)

FLOPS = 2 * K * C * N

F32, BF16, U16 = mybir.dt.float32, mybir.dt.bfloat16, mybir.dt.uint16
ADD, MULT = mybir.AluOpType.add, mybir.AluOpType.mult
LINEAR = mybir.ActivationFunctionType.Identity


def tile_reledgeupdate_kernel(tc, self_h, src_e, w, b, wa_z, wa_s, offs, out):
    nc = tc.nc
    with tc.tile_pool(name="held", bufs=1) as held:
        offsets = held.tile([P, N // PER_COLUMN], U16, name="offsets")
        sizes_of = [HEAD, (PIECE, PIECE) + TAPER]
        pieces_of = [[(sum(sizes[:i]), size) for i, size in enumerate(sizes)] for sizes in sizes_of]
        w_sb = held.tile([K, C], BF16, name="w_sb")
        nc.sync.dma_start(w_sb[:, 0:P], w[:, 0:P])
        src_sb = held.tile([K, N], BF16, name="src_sb")
        chunks = [(sum(CHUNKS[:i]), size) for i, size in enumerate(CHUNKS)]
        raw = [held.tile([P, S], F32, name=f"raw{t}") for t in range(BLOCKS)]
        nc.sync.dma_start(src_sb[:, 0 : HEAD[0]], src_e[:, 0 : HEAD[0]])
        rows = held.tile([P, BLOCKS * TURN], F32, name="rows", align_bytes=64)
        nc.vector.memset(rows[:], 0.0)
        by_block = rows[:].rearrange("(q r) (t j) -> q r t j", r=TURN, j=TURN)
        for v, param in enumerate((b, wa_z, wa_s)):
            nc.sync.dma_start(
                by_block[:, v], param.rearrange("(t q j) o -> q t (j o)", t=BLOCKS, j=TURN)
            )
        for node, size in chunks:
            nc.sync.dma_start(raw[0][:, node : node + size], self_h[0:P, node : node + size])
        nc.sync.dma_start(offsets[:], offs)
        for first, size in pieces_of[0][1:]:
            nc.sync.dma_start(src_sb[:, first : first + size], src_e[:, first : first + size])
        nc.sync.dma_start(w_sb[:, P:C], w[:, P:C])
        for node, size in chunks:
            nc.sync.dma_start(raw[1][:, node : node + size], self_h[P : 2 * P, node : node + size])

        turned = []
        for t in range(BLOCKS):
            columns = held.tile([P, TURN], F32, name=f"turned{t}", align_bytes=64)
            nc.vector.transpose(columns[:], rows[:, t * TURN : (t + 1) * TURN])
            turned.append(columns)
        wa_z_col = [columns[:, 1:2] for columns in turned]
        wa_s_col = [columns[:, 2:3] for columns in turned]
        b_wa_z = [held.tile([P, 1], F32, name=f"b_wa_z{t}") for t in range(BLOCKS)]
        for t in range(BLOCKS):
            nc.scalar.activation(b_wa_z[t][:], turned[t][:, 0:1], LINEAR, scale=wa_z_col[t])

        with tc.psum_pool(name="banks", bufs=4) as banks:
            zt = [held.tile([P, N], F32, name=f"zt{t}") for t in range(BLOCKS)]

            def project(t, edge, width):
                bank = banks.tile([P, BANK], F32, name="bank")
                nc.tensor.matmul(
                    bank[:, 0:width],
                    w_sb[:, t * P : (t + 1) * P],
                    src_sb[:, edge : edge + width],
                    start=True,
                    stop=True,
                )
                return bank

            def scale_on_scalar(t, edge, width, bank):
                nc.scalar.activation(
                    zt[t][:, edge : edge + width],
                    bank[:, 0:width],
                    LINEAR,
                    bias=b_wa_z[t][:],
                    scale=wa_z_col[t],
                )

            widths = [
                (first + col, min(BANK, size - col))
                for first, size in pieces_of[0]
                for col in range(0, size, BANK)
            ]
            edge, width = widths[0]
            bank = project(0, edge, width)
            nc.vector.tensor_scalar(
                zt[0][:, edge : edge + width],
                bank[:, 0:width],
                turned[0][:, 0:1],
                wa_z_col[0],
                ADD,
                MULT,
            )

            for t in range(BLOCKS):
                hs = held.tile([P, S], F32, name=f"hs{t}")
                for node, size in chunks:
                    if t == 0:
                        nc.vector.tensor_scalar(
                            hs[:, node : node + size],
                            raw[t][:, node : node + size],
                            wa_s_col[t],
                            None,
                            MULT,
                        )
                    else:
                        nc.scalar.activation(
                            hs[:, node : node + size],
                            raw[t][:, node : node + size],
                            LINEAR,
                            scale=wa_s_col[t],
                        )

                for edge, width in widths if t else widths[1:]:
                    scale_on_scalar(t, edge, width, project(t, edge, width))

                total = held.tile([P, N], F32, name=f"total{t}")
                for first, size in pieces_of[t]:
                    piece_offsets = offsets[:, first // PER_COLUMN : (first + size) // PER_COLUMN]
                    nc.vector.tensor_tensor(
                        total[:, first : first + size],
                        hs[:].indirect(piece_offsets),
                        zt[t][:, first : first + size],
                        ADD,
                    )
                    nc.sync.dma_start(
                        out[t * P : (t + 1) * P, first : first + size],
                        total[:, first : first + size],
                    )
